import numpy as np
import ml_dtypes


def mxq(x, axis, fmt="e4m3"):
    dtype, down = {"e4m3": (ml_dtypes.float8_e4m3fn, 7), "e5m2": (ml_dtypes.float8_e5m2, 14)}[fmt]
    v = np.moveaxis(np.asarray(x, np.float32).astype(ml_dtypes.bfloat16).astype(np.float64), axis, -1)
    blocks = v.reshape(v.shape[:-1] + (-1, 32))
    amax = np.abs(blocks).max(-1, keepdims=True)
    byte = np.maximum(np.where(amax > 0, np.frexp(amax)[1] - 1 + 127, 0) - down, 1)
    scale = np.exp2(byte - 127.0)
    codes = (blocks / scale).astype(np.float32).astype(dtype).astype(np.float64)
    return np.moveaxis((codes * scale).reshape(v.shape), -1, axis)


WIDE = False


def mx_kscale(k):
    if not WIDE:
        return np.ones(k)
    levels = np.array([10, -10, 5, -5, 0])
    if k % 512:
        return np.exp2(np.random.permutation(np.resize(levels, k // 32))).repeat(32)
    a = np.empty((k // 512, 16))
    for p in range(k // 512):
        a[p, :8] = np.random.permutation(np.resize(levels, 8))
        for g in range(8):
            far = levels[np.abs(levels - a[p, g]) >= 10]
            a[p, g + 8] = far[np.random.randint(len(far))]
    return np.exp2(a.ravel()).repeat(32)


BF16 = ml_dtypes.bfloat16


def bf(x):
    return np.asarray(x, np.float32).astype(BF16)


def f64(x):
    return np.asarray(x).astype(np.float64)


N, I, O = 8192, 512, 128


def draw0():
    s = mx_kscale(I)
    mask = np.tile(np.array([0.0, 0.0, 1.0, 1.0]), I // 4)
    gd = mask + 0.1 * (1.0 - mask)
    gs = (1.0 - mask) + 0.1 * mask
    x = np.random.standard_normal((N, I)) * s
    wd = np.random.standard_normal((O, I)) * gd / np.sqrt(I) / s
    ws = np.random.standard_normal((O, I)) * gs / np.sqrt(I) / s
    return {"x": bf(x), "W_dense": bf(wd), "W_sparse": bf(ws)}


def core(x, W_dense, W_sparse):
    xq = mxq(f64(x), 1, "e4m3")
    out_dense = xq @ mxq(f64(W_dense), 1, "e4m3").T
    out_sparse = xq @ mxq(f64(W_sparse), 1, "e4m3").T
    return out_dense + out_sparse


def e4m3fn_bytes(y):
    return np.clip(np.asarray(y, np.float64), -448.0, 448.0).astype(np.float32).astype(ml_dtypes.float8_e4m3fn).view(np.uint8)


def e4m3fn_values(b):
    return np.asarray(b, np.uint8).view(ml_dtypes.float8_e4m3fn).astype(np.float64)


def setup_inputs():
    d = draw0()
    x0 = np.asarray(d['x']).astype(np.float64)
    s = (np.max(np.abs(x0), axis=(0,), keepdims=True) / 448.0).astype(np.float32)
    out = {}
    for k, v in d.items():
        if k == 'x':
            out['x_bytes'] = e4m3fn_bytes(x0 / s.astype(np.float64))
            out['x_scale'] = s
        else:
            out[k] = v
    return out


def reference(x_bytes, x_scale, W_dense, W_sparse):
    return core(e4m3fn_values(x_bytes) * x_scale.astype(np.float64), W_dense, W_sparse)

@@ -1,0 +1,263 @@
+from contextlib import ExitStack
+
+import concourse.mybir as mybir
+from concourse.masks import make_identity
+
+ROWS, K, O = 8192, 512, 128
+FLOPS = 2 * 2 * ROWS * K * O
+
+F32 = mybir.dt.float32
+BF16 = mybir.dt.bfloat16
+U32 = mybir.dt.uint32
+U8 = mybir.dt.uint8
+FP8 = mybir.dt.float8_e4m3fn
+FP8X4 = mybir.dt.float8_e4m3fn_x4
+COPY = mybir.ActivationFunctionType.Copy
+
+P = 128
+TILES = ROWS // P
+WORDS = K // 2
+MAXT = 4
+
+UNITS = 6
+VCAST = 2
+FIRST = 2 * UNITS
+LOADS = [(0, 2), (2, 2), (12, 2), (4, 4), (14, 2)] + [(8, 4), (16, 8), (24, 8), (32, 8), (40, 8), (48, 8), (56, 8)]
+W_AFTER = 4
+CHUNKS = [4] * 12 + [2,1,1]
+TAPER = 3
+LAG = 3
+LATE_LAGS = [3, 3, 3, 3, 0]
+PIECE = {0: 1, 1: 2}
+TAILFIX = True
+
+
+def tile_myinterleavedmodule_t_kernel(tc, x_bytes, x_scale, W_dense, W_sparse, out):
+    nc = tc.nc
+    x_rows = x_bytes.rearrange("(p j) k -> p (j k)", j=TILES)
+    out_rows = out.rearrange("(p j) o -> p (j o)", j=TILES)
+
+    with ExitStack() as ctx:
+        const = ctx.enter_context(tc.tile_pool(name="const", bufs=1))
+        held = ctx.enter_context(tc.tile_pool(name="held", bufs=1))
+        wide = ctx.enter_context(tc.tile_pool(name="wide", bufs=4))
+        castp = ctx.enter_context(tc.tile_pool(name="castp", bufs=4))
+        planes = ctx.enter_context(tc.tile_pool(name="planes", bufs=2))
+        grp = ctx.enter_context(tc.tile_pool(name="grp", bufs=6))
+        mxp = ctx.enter_context(tc.tile_pool(name="mxp", bufs=3))
+        resp = ctx.enter_context(tc.tile_pool(name="resp", bufs=8))
+        psum_t = ctx.enter_context(tc.psum_pool(name="psum_t", bufs=4))
+        psum_u = ctx.enter_context(tc.psum_pool(name="psum_u", bufs=2))
+        psum_o = ctx.enter_context(tc.psum_pool(name="psum_o", bufs=2))
+
+        ident = const.tile([P, P], F32, name="ident")
+        make_identity(nc, ident[:])
+
+        scales4 = const.tile([P, MAXT * K], F32, name="scales4")
+        nc.scalar.dma_start(out=scales4[:, 0:K], in_=x_scale.rearrange("o k -> (o k)").partition_broadcast(P))
+        scale_cols = const.tile([P, 4], F32, name="scale_cols")
+        nc.scalar.dma_start(out=scale_cols[:], in_=x_scale.rearrange("o (p t) -> p (o t)", t=4))
+        warm = const.tile([P, 1], F32, name="warm")
+        nc.scalar.activation(out=warm[:], in_=ident[:, 0:1], func=COPY)
+
+        w_sb = const.tile([P, 2 * K], BF16, name="w_sb")
+        byte_tiles = []
+        for g, (start, n) in enumerate(LOADS):
+            xb = held.tile([P, n * K], U8, name="xbytes%d" % g)
+            nc.sync.dma_start(out=xb[:], in_=x_rows[:, start * K:(start + n) * K])
+            byte_tiles.append((start, n, xb))
+            if g == W_AFTER:
+                nc.sync.dma_start(out=w_sb[:, 0:K], in_=W_dense)
+                nc.sync.dma_start(out=w_sb[:, K:2 * K], in_=W_sparse)
+
+        def bytes_of(j0, n):
+            for s, m, xb in byte_tiles:
+                if s <= j0 and j0 + n <= s + m:
+                    return xb[:, (j0 - s) * K:(j0 - s + n) * K]
+            raise ValueError("chunk crosses a load")
+
+        def turn_bank(xt, words, j0, nb):
+            for jl in range(nb):
+                base = (j0 + jl) * WORDS
+                for u in range(2):
+                    nc.tensor.transpose(xt[:, jl, u, :], words[:, base + u:base + WORDS:2], ident[:])
+
+        def turn(src, n):
+            words = src[:, 0:n * K].bitcast(F32)
+            banks = []
+            for b0 in range(0, n, 2):
+                nb = min(2, n - b0)
+                xt = psum_t.tile([P, 2, 2, P], F32, name="xt", tag="xt")
+                turn_bank(xt, words, b0, nb)
+                banks.append((b0, nb, xt))
+            return banks
+
+        def gather(banks, grouped):
+            gw = grouped[:].bitcast(F32).rearrange("p (j r u) -> p j r u", r=P, u=2)
+            for b0, nb, xt in banks:
+                nc.scalar.copy(out=gw[:, b0:b0 + nb], in_=xt[:, 0:nb].rearrange("p j u r -> p j r u"))
+
+        def quantize(grouped, codes, scl, n):
+            nc.vector.quantize_mx(
+                out=codes[:, 0:n * P].bitcast(FP8X4), scales=scl[:, 0:n * P], in_=grouped[:, 0:n * K]
+            )
+
+        w_grouped = const.tile([P, 2 * K], BF16, name="w_grouped", align_bytes=64)
+        w_codes = const.tile([P, 2 * P], U32, name="w_codes", align_bytes=64)
+        w_scl = const.tile([P, 2 * P], U8, name="w_scl", align_bytes=64)
+
+        starts = []
+        start = FIRST
+        for n in CHUNKS:
+            starts.append(start)
+            start += n
+        nchunks = len(CHUNKS)
+        state = {}
+
+        def stage_a(i):
+            n = CHUNKS[i]
+            step = min(n, PIECE.get(i, MAXT))
+            xbf = wide.tile([P, MAXT * K], BF16, name="xbf", tag="xbf")
+            for a in range(0, n, step):
+                nc.vector.tensor_tensor(
+                    out=xbf[:, a * K:(a + step) * K],
+                    in0=bytes_of(starts[i] + a, step).bitcast(FP8),
+                    in1=scales4[:, 0:step * K],
+                    op=mybir.AluOpType.mult,
+                )
+            state[("xbf", i)] = xbf
+
+        def stage_b(i):
+            state[("banks", i)] = turn(state[("xbf", i)], CHUNKS[i])
+
+        def stage_c(i):
+            grouped = grp.tile([P, MAXT * K], BF16, name="grouped", tag="grouped", align_bytes=64)
+            gather(state[("banks", i)], grouped)
+            state[("grouped", i)] = grouped
+
+        def multiply(grouped, n, spare_bank):
+            codes = mxp.tile([P, MAXT * P], U32, name="codes", tag="codes", align_bytes=64)
+            scl = mxp.tile([P, MAXT * P], U8, name="scl", tag="scl", align_bytes=64)
+            quantize(grouped, codes, scl, n)
+            if spare_bank:
+                acc = psum_u.tile([P, MAXT, O], F32, name="ut", tag="ut")
+            else:
+                acc = psum_o.tile([P, MAXT, O], F32, name="acc", tag="acc")
+            for jl in range(n):
+                cols = slice(jl * P, (jl + 1) * P)
+                for w in range(2):
+                    nc.tensor.matmul_mx(
+                        out=acc[:, jl, :],
+                        lhsT=codes[:, cols].bitcast(FP8X4),
+                        lhsT_scale=scl[:, cols],
+                        rhs=w_codes[:, w * O:(w + 1) * O].bitcast(FP8X4),
+                        rhs_scale=w_scl[:, w * O:(w + 1) * O],
+                        start=(w == 0),
+                        stop=(w == 1),
+                    )
+            return acc
+
+        def store(acc, j0, n, on_vector):
+            res = resp.tile([P, MAXT * O], F32, name="res", tag="res")
+            if on_vector:
+                nc.vector.tensor_copy(out=res[:, 0:n * O], in_=acc[:, 0:n, :].rearrange("p j o -> p (j o)"))
+            else:
+                nc.scalar.copy(out=res[:, 0:n * O], in_=acc[:, 0:n, :].rearrange("p j o -> p (j o)"))
+            nc.sync.dma_start(out=out_rows[:, j0 * O:(j0 + n) * O], in_=res[:, 0:n * O])
+
+        def finish(grouped, j0, n):
+            store(multiply(grouped, n, False), j0, n, False)
+
+        def u_cast(q):
+            xc = castp.tile([P, 2 * K], BF16, name="xc", tag="xc")
+            if q < VCAST:
+                nc.vector.tensor_copy(out=xc[:], in_=bytes_of(2 * q, 2).bitcast(FP8))
+            else:
+                nc.scalar.copy(out=xc[:], in_=bytes_of(2 * q, 2).bitcast(FP8))
+            state[("xc", q)] = xc
+
+        def u_turn(q):
+            ut = psum_u.tile([P, 2, 2, P], F32, name="ut", tag="ut")
+            turn_bank(ut, state[("xc", q)][:].bitcast(F32), 0, 2)
+            state[("ut", q)] = ut
+
+        def u_tiles(c):
+            return min(MAXT, FIRST - MAXT * c)
+
+        def u_scale(q, t):
+            c = q // 2
+            if q % 2 == 0 and t == 0:
+                pl = planes.tile([P, MAXT * K], BF16, name="pl", tag="pl")
+                state[("pl", c)] = pl
+            nj = u_tiles(c)
+            pl = state[("pl", c)]
+            u, e = divmod(t, 2)
+            j0 = 2 * (q % 2)
+            src = state[("ut", q)][:].rearrange("p j u r -> p (j u r)").bitcast(BF16)
+            src = src.rearrange("p (j u r e) -> p j u r e", j=2, u=2, e=2)
+            dst = pl[:, 0:nj * K].rearrange("p (u j r e) -> p u j r e", u=2, j=nj, e=2)
+            nc.scalar.activation(
+                out=dst[:, u, j0:j0 + 2, :, e], in_=src[:, :, u, :, e], func=COPY, scale=scale_cols[:, t:t + 1]
+            )
+
+        def u_weave(c):
+            nj = u_tiles(c)
+            grouped = grp.tile([P, MAXT * K], BF16, name="grouped", tag="grouped", align_bytes=64)
+            nc.vector.tensor_copy(
+                out=grouped[:, 0:nj * K].bitcast(F32).rearrange("p (j r u) -> p j r u", r=P, u=2),
+                in_=state[("pl", c)][:, 0:nj * K].bitcast(F32).rearrange("p (u j r) -> p j r u", u=2, r=P),
+            )
+            state[("woven", c)] = grouped
+
+        ctx.enter_context(tc.manual_schedule())
+
+        u_cast(0)
+        u_turn(0)
+        u_cast(1)
+        u_turn(1)
+        u_cast(2)
+        w_banks = turn(w_sb, 2)
+        nc.scalar.copy(out=scales4[:, K:2 * K], in_=scales4[:, 0:K])
+        nc.scalar.copy(out=scales4[:, 2 * K:4 * K], in_=scales4[:, 0:2 * K])
+        for t in range(4):
+            u_scale(0, t)
+        gather(w_banks, w_grouped)
+
+        weave_at = {}
+        for c in range((UNITS + 1) // 2):
+            last_unit = min(2 * c + 1, UNITS - 1)
+            weave_at[max(2 * last_unit + 2, 4)] = c
+
+        done = 0
+        for i in range(nchunks + 1):
+            if i in weave_at:
+                u_weave(weave_at[i])
+            if i < nchunks:
+                stage_a(i)
+                stage_b(i)
+                stage_c(i)
+            q = 1 + i // 2
+            if q < UNITS:
+                u_scale(q, 2 * (i % 2))
+                u_scale(q, 2 * (i % 2) + 1)
+            q = (i + 5) // 2
+            if i % 2 == 1 and 3 <= q < UNITS:
+                u_cast(q)
+            q = (i + 3) // 2
+            if i % 2 == 1 and 2 <= q < UNITS:
+                u_turn(q)
+            if i == LAG:
+                quantize(w_grouped, w_codes, w_scl, 2)
+            if i in weave_at:
+                c = weave_at[i]
+                finish(state[("woven", c)], MAXT * c, u_tiles(c))
+            lag = LAG if i < nchunks - TAPER - 1 else LATE_LAGS[i - (nchunks - TAPER - 1)]
+            late = []
+            while done < nchunks and done <= i - lag:
+                if TAILFIX and done >= nchunks - 2:
+                    late.append((multiply(state[("grouped", done)], CHUNKS[done], True), starts[done], CHUNKS[done]))
+                else:
+                    finish(state[("grouped", done)], starts[done], CHUNKS[done])
+                done += 1
+            for acc, j0, n in late:
+                store(acc, j0, n, True)

@@ -22,8 +22,9 @@ MAXT = 4
 UNITS = 6
 VCAST = 2
 FIRST = 2 * UNITS
-LOADS = [(0, 2), (2, 2), (12, 2), (4, 4), (14, 2)] + [(8, 4), (16, 8), (24, 8), (32, 8), (40, 8), (48, 8), (56, 8)]
+LOADS = [(0, 2), (2, 2), (12, 2), (4, 4), (14, 2), (16, 4)] + [(20, 4), (8, 4), (24, 8), (32, 8), (40, 8), (48, 8), (56, 8)]
 W_AFTER = 4
+REPEAT_AFTER = 5
 CHUNKS = [4] * 12 + [2,1,1]
 TAPER = 3
 LAG = 3
@@ -50,6 +51,8 @@ def tile_myinterleavedmodule_t_kernel(tc, x_bytes, x_scale, W_dense, W_sparse, o
         psum_u = ctx.enter_context(tc.psum_pool(name="psum_u", bufs=2))
         psum_o = ctx.enter_context(tc.psum_pool(name="psum_o", bufs=2))
 
+        ctx.enter_context(tc.manual_schedule())
+
         ident = const.tile([P, P], F32, name="ident")
         make_identity(nc, ident[:])
 
@@ -66,6 +69,9 @@ def tile_myinterleavedmodule_t_kernel(tc, x_bytes, x_scale, W_dense, W_sparse, o
             xb = held.tile([P, n * K], U8, name="xbytes%d" % g)
             nc.sync.dma_start(out=xb[:], in_=x_rows[:, start * K:(start + n) * K])
             byte_tiles.append((start, n, xb))
+            if g == REPEAT_AFTER:
+                for rcopy in range(1, MAXT):
+                    nc.sync.dma_start(out=scales4[:, rcopy * K:(rcopy + 1) * K], in_=scales4[:, 0:K])
             if g == W_AFTER:
                 nc.sync.dma_start(out=w_sb[:, 0:K], in_=W_dense)
                 nc.sync.dma_start(out=w_sb[:, K:2 * K], in_=W_sparse)
@@ -203,13 +209,11 @@ def tile_myinterleavedmodule_t_kernel(tc, x_bytes, x_scale, W_dense, W_sparse, o
         def u_weave(c):
             nj = u_tiles(c)
             grouped = grp.tile([P, MAXT * K], BF16, name="grouped", tag="grouped", align_bytes=64)
-            nc.vector.tensor_copy(
+            nc.scalar.copy(
                 out=grouped[:, 0:nj * K].bitcast(F32).rearrange("p (j r u) -> p j r u", r=P, u=2),
                 in_=state[("pl", c)][:, 0:nj * K].bitcast(F32).rearrange("p (u j r) -> p j r u", u=2, r=P),
             )
             state[("woven", c)] = grouped
-
-        ctx.enter_context(tc.manual_schedule())
 
         u_cast(0)
         u_turn(0)
@@ -217,8 +221,6 @@ def tile_myinterleavedmodule_t_kernel(tc, x_bytes, x_scale, W_dense, W_sparse, o
         u_turn(1)
         u_cast(2)
         w_banks = turn(w_sb, 2)
-        nc.scalar.copy(out=scales4[:, K:2 * K], in_=scales4[:, 0:K])
-        nc.scalar.copy(out=scales4[:, 2 * K:4 * K], in_=scales4[:, 0:2 * K])
         for t in range(4):
             u_scale(0, t)
         gather(w_banks, w_grouped)
@@ -226,16 +228,16 @@ def tile_myinterleavedmodule_t_kernel(tc, x_bytes, x_scale, W_dense, W_sparse, o
         weave_at = {}
         for c in range((UNITS + 1) // 2):
             last_unit = min(2 * c + 1, UNITS - 1)
-            weave_at[max(2 * last_unit + 2, 4)] = c
+            weave_at[2 * last_unit + 3] = c
 
         done = 0
         for i in range(nchunks + 1):
-            if i in weave_at:
-                u_weave(weave_at[i])
             if i < nchunks:
                 stage_a(i)
                 stage_b(i)
                 stage_c(i)
+            if i + LAG in weave_at:
+                u_weave(weave_at[i + LAG])
             q = 1 + i // 2
             if q < UNITS:
                 u_scale(q, 2 * (i % 2))

@@ -127,8 +127,8 @@ def tile_myinterleavedmodule_t_kernel(tc, x_bytes, x_scale, W_dense, W_sparse, o
             for a in range(0, n, step):
                 nc.vector.tensor_tensor(
                     out=xbf[:, a * K:(a + step) * K],
-                    in0=bytes_of(starts[i] + a, step).bitcast(FP8),
-                    in1=scales4[:, 0:step * K],
+                    in0=scales4[:, 0:step * K],
+                    in1=bytes_of(starts[i] + a, step).bitcast(FP8),
                     op=mybir.AluOpType.mult,
                 )
             state[("xbf", i)] = xbf

@@ -20,7 +20,7 @@ WORDS = K // 2
 MAXT = 4
 
 UNITS = 6
-VCAST = 2
+VCAST = 3
 FIRST = 2 * UNITS
 LOADS = [(0, 2), (2, 2), (12, 2), (4, 4), (14, 2), (16, 4)] + [(20, 4), (8, 4), (24, 8), (32, 8), (40, 8), (48, 8), (56, 8)]
 W_AFTER = 4
@@ -219,7 +219,6 @@ def tile_myinterleavedmodule_t_kernel(tc, x_bytes, x_scale, W_dense, W_sparse, o
         u_turn(0)
         u_cast(1)
         u_turn(1)
-        u_cast(2)
         w_banks = turn(w_sb, 2)
         for t in range(4):
             u_scale(0, t)
@@ -234,6 +233,8 @@ def tile_myinterleavedmodule_t_kernel(tc, x_bytes, x_scale, W_dense, W_sparse, o
         for i in range(nchunks + 1):
             if i < nchunks:
                 stage_a(i)
+                if i == 0:
+                    u_cast(2)
                 stage_b(i)
                 stage_c(i)
             if i + LAG in weave_at:

@@ -12,25 +12,22 @@ U32 = mybir.dt.uint32
 U8 = mybir.dt.uint8
 FP8 = mybir.dt.float8_e4m3fn
 FP8X4 = mybir.dt.float8_e4m3fn_x4
+
 COPY = mybir.ActivationFunctionType.Copy
+MULT = mybir.AluOpType.mult
+ADD = mybir.AluOpType.add
 
 P = 128
 TILES = ROWS // P
-WORDS = K // 2
-MAXT = 4
+PAIRS = TILES // 2
 
-UNITS = 6
-VCAST = 3
-FIRST = 2 * UNITS
-LOADS = [(0, 2), (2, 2), (12, 2), (4, 4), (14, 2), (16, 4)] + [(20, 4), (8, 4), (24, 8), (32, 8), (40, 8), (48, 8), (56, 8)]
-W_AFTER = 4
-REPEAT_AFTER = 5
-CHUNKS = [4] * 12 + [2,1,1]
-TAPER = 3
-LAG = 3
-LATE_LAGS = [3, 3, 3, 3, 0]
-PIECE = {0: 1, 1: 2}
-TAILFIX = True
+CASTS = ["V","S","S","S","S","S","S","S","S","S","S","S","S","S","S","S","S","S","S","S","S","S","S","S","S","S","S","S","S","S","S","S"]
+ROADS = ["p","e","p","e","p","e","p","f","p","e","p","e","p","e","p","f","p","e","p","e","p","e","p","f","p","e","p","e","p","e","p","p"]
+LOADS = [(0, 2), (2, 2), (4, 4), (8, 8), (16, 8), (24, 8), (32, 8), (40, 8), (48, 8), (56, 8)]
+W_AFTER = 2
+LAG = 2
+AHEAD = 4
+CHUNKS = [2] * 15 + [1, 1]
 
 
 def tile_myinterleavedmodule_t_kernel(tc, x_bytes, x_scale, W_dense, W_sparse, out):
@@ -41,25 +38,24 @@ def tile_myinterleavedmodule_t_kernel(tc, x_bytes, x_scale, W_dense, W_sparse, o
     with ExitStack() as ctx:
         const = ctx.enter_context(tc.tile_pool(name="const", bufs=1))
         held = ctx.enter_context(tc.tile_pool(name="held", bufs=1))
-        wide = ctx.enter_context(tc.tile_pool(name="wide", bufs=4))
-        castp = ctx.enter_context(tc.tile_pool(name="castp", bufs=4))
-        planes = ctx.enter_context(tc.tile_pool(name="planes", bufs=2))
-        grp = ctx.enter_context(tc.tile_pool(name="grp", bufs=6))
+        castp = ctx.enter_context(tc.tile_pool(name="castp", bufs=6))
+        planep = ctx.enter_context(tc.tile_pool(name="planep", bufs=4))
+        grp = ctx.enter_context(tc.tile_pool(name="grp", bufs=5))
         mxp = ctx.enter_context(tc.tile_pool(name="mxp", bufs=3))
-        resp = ctx.enter_context(tc.tile_pool(name="resp", bufs=8))
-        psum_t = ctx.enter_context(tc.psum_pool(name="psum_t", bufs=4))
-        psum_u = ctx.enter_context(tc.psum_pool(name="psum_u", bufs=2))
-        psum_o = ctx.enter_context(tc.psum_pool(name="psum_o", bufs=2))
+        resp = ctx.enter_context(tc.tile_pool(name="resp", bufs=6))
+        psum_t = ctx.enter_context(tc.psum_pool(name="psum_t", bufs=5))
+        psum_o = ctx.enter_context(tc.psum_pool(name="psum_o", bufs=3))
 
         ctx.enter_context(tc.manual_schedule())
 
         ident = const.tile([P, P], F32, name="ident")
         make_identity(nc, ident[:])
+        ident_b = const.tile([P, P], BF16, name="ident_b")
+        nc.vector.tensor_copy(out=ident_b[:], in_=ident[:])
 
-        scales4 = const.tile([P, MAXT * K], F32, name="scales4")
-        nc.scalar.dma_start(out=scales4[:, 0:K], in_=x_scale.rearrange("o k -> (o k)").partition_broadcast(P))
-        scale_cols = const.tile([P, 4], F32, name="scale_cols")
-        nc.scalar.dma_start(out=scale_cols[:], in_=x_scale.rearrange("o (p t) -> p (o t)", t=4))
+        scale_cols = const.tile([P, 1, 2, 2], F32, name="scale_cols")
+        nc.scalar.dma_start(out=scale_cols[:].rearrange("p o u e -> p (o u e)"), in_=x_scale.rearrange("o (p t) -> p (o t)", t=4))
+        flat_cols = scale_cols[:].rearrange("p o u e -> p (o u e)")
         warm = const.tile([P, 1], F32, name="warm")
         nc.scalar.activation(out=warm[:], in_=ident[:, 0:1], func=COPY)
 
@@ -69,9 +65,6 @@ def tile_myinterleavedmodule_t_kernel(tc, x_bytes, x_scale, W_dense, W_sparse, o
             xb = held.tile([P, n * K], U8, name="xbytes%d" % g)
             nc.sync.dma_start(out=xb[:], in_=x_rows[:, start * K:(start + n) * K])
             byte_tiles.append((start, n, xb))
-            if g == REPEAT_AFTER:
-                for rcopy in range(1, MAXT):
-                    nc.sync.dma_start(out=scales4[:, rcopy * K:(rcopy + 1) * K], in_=scales4[:, 0:K])
             if g == W_AFTER:
                 nc.sync.dma_start(out=w_sb[:, 0:K], in_=W_dense)
                 nc.sync.dma_start(out=w_sb[:, K:2 * K], in_=W_sparse)
@@ -80,28 +73,22 @@ def tile_myinterleavedmodule_t_kernel(tc, x_bytes, x_scale, W_dense, W_sparse, o
             for s, m, xb in byte_tiles:
                 if s <= j0 and j0 + n <= s + m:
                     return xb[:, (j0 - s) * K:(j0 - s + n) * K]
-            raise ValueError("chunk crosses a load")
+            raise ValueError("pair crosses a load")
 
-        def turn_bank(xt, words, j0, nb):
-            for jl in range(nb):
-                base = (j0 + jl) * WORDS
+        def turn_words(src):
+            words = src.bitcast(F32)
+            bank = psum_t.tile([P, 2, 2, P], F32, name="bank", tag="bank")
+            for j in range(2):
                 for u in range(2):
-                    nc.tensor.transpose(xt[:, jl, u, :], words[:, base + u:base + WORDS:2], ident[:])
+                    nc.tensor.transpose(bank[:, u, j, :], words[:, j * 256 + u:(j + 1) * 256:2], ident[:])
+            return bank
 
-        def turn(src, n):
-            words = src[:, 0:n * K].bitcast(F32)
-            banks = []
-            for b0 in range(0, n, 2):
-                nb = min(2, n - b0)
-                xt = psum_t.tile([P, 2, 2, P], F32, name="xt", tag="xt")
-                turn_bank(xt, words, b0, nb)
-                banks.append((b0, nb, xt))
-            return banks
-
-        def gather(banks, grouped):
-            gw = grouped[:].bitcast(F32).rearrange("p (j r u) -> p j r u", r=P, u=2)
-            for b0, nb, xt in banks:
-                nc.scalar.copy(out=gw[:, b0:b0 + nb], in_=xt[:, 0:nb].rearrange("p j u r -> p j r u"))
+        def turn_values(src):
+            bank = psum_t.tile([P, 4, 2, P], BF16, name="bankb", tag="bank")
+            for j in range(2):
+                for t in range(4):
+                    nc.tensor.transpose(bank[:, t, j, :], src[:, j * K + t:(j + 1) * K:4], ident_b[:])
+            return bank
 
         def quantize(grouped, codes, scl, n):
             nc.vector.quantize_mx(
@@ -112,44 +99,63 @@ def tile_myinterleavedmodule_t_kernel(tc, x_bytes, x_scale, W_dense, W_sparse, o
         w_codes = const.tile([P, 2 * P], U32, name="w_codes", align_bytes=64)
         w_scl = const.tile([P, 2 * P], U8, name="w_scl", align_bytes=64)
 
-        starts = []
-        start = FIRST
-        for n in CHUNKS:
-            starts.append(start)
-            start += n
-        nchunks = len(CHUNKS)
         state = {}
 
-        def stage_a(i):
-            n = CHUNKS[i]
-            step = min(n, PIECE.get(i, MAXT))
-            xbf = wide.tile([P, MAXT * K], BF16, name="xbf", tag="xbf")
-            for a in range(0, n, step):
-                nc.vector.tensor_tensor(
-                    out=xbf[:, a * K:(a + step) * K],
-                    in0=scales4[:, 0:step * K],
-                    in1=bytes_of(starts[i] + a, step).bitcast(FP8),
-                    op=mybir.AluOpType.mult,
-                )
-            state[("xbf", i)] = xbf
-
-        def stage_b(i):
-            state[("banks", i)] = turn(state[("xbf", i)], CHUNKS[i])
-
-        def stage_c(i):
-            grouped = grp.tile([P, MAXT * K], BF16, name="grouped", tag="grouped", align_bytes=64)
-            gather(state[("banks", i)], grouped)
-            state[("grouped", i)] = grouped
-
-        def multiply(grouped, n, spare_bank):
-            codes = mxp.tile([P, MAXT * P], U32, name="codes", tag="codes", align_bytes=64)
-            scl = mxp.tile([P, MAXT * P], U8, name="scl", tag="scl", align_bytes=64)
-            quantize(grouped, codes, scl, n)
-            if spare_bank:
-                acc = psum_u.tile([P, MAXT, O], F32, name="ut", tag="ut")
+        def cast(q):
+            xc = castp.tile([P, 2 * K], BF16, name="xc", tag="xc")
+            src = bytes_of(2 * q, 2).bitcast(FP8)
+            if CASTS[q] == "S":
+                nc.scalar.copy(out=xc[:], in_=src)
+            elif CASTS[q] == "G":
+                for h in range(2):
+                    nc.gpsimd.tensor_copy(out=xc[:, h * K:(h + 1) * K], in_=src[:, h * K:(h + 1) * K])
             else:
-                acc = psum_o.tile([P, MAXT, O], F32, name="acc", tag="acc")
-            for jl in range(n):
+                nc.vector.tensor_copy(out=xc[:], in_=src)
+            state[("xc", q)] = xc
+
+        def turn(q):
+            xc = state[("xc", q)]
+            state[("bank", q)] = turn_values(xc[:]) if ROADS[q] == "e" else turn_words(xc[:])
+
+        def scale(q):
+            bank = state[("bank", q)]
+            grouped, g0 = state[("place", q)]
+            dst = grouped[:, g0 * 2 * K:(g0 + 1) * 2 * K]
+            if ROADS[q] == "p":
+                src = bank[:].rearrange("p u j r -> p (u j r)").bitcast(BF16)
+                nc.vector.tensor_tensor(
+                    out=dst.rearrange("p (m u e) -> p m u e", u=2, e=2),
+                    in0=src.rearrange("p (u m e) -> p m u e", u=2, e=2),
+                    in1=scale_cols[:].to_broadcast([P, 2 * P, 2, 2]),
+                    op=MULT,
+                )
+                return
+            pl = planep.tile([P, 4, 2 * P], BF16, name="pl", tag="pl")
+            if ROADS[q] == "e":
+                for t in range(4):
+                    nc.vector.tensor_scalar(
+                        out=pl[:, t, :], in0=bank[:, t].rearrange("p j r -> p (j r)"),
+                        scalar1=flat_cols[:, t:t + 1], scalar2=None, op0=MULT,
+                    )
+            else:
+                src = bank[:].rearrange("p u j r -> p (u j r)").bitcast(BF16)
+                src = src.rearrange("p (u m e) -> p u e m", u=2, e=2)
+                for t in range(4):
+                    nc.scalar.activation(out=pl[:, t, :], in_=src[:, t // 2, t % 2, :], func=COPY, scale=flat_cols[:, t:t + 1])
+            for h in range(2):
+                nc.gpsimd.tensor_scalar(
+                    out=dst[:, h * K:(h + 1) * K].rearrange("p (r t) -> p r t", t=4),
+                    in0=pl[:, :, h * P:(h + 1) * P].rearrange("p t r -> p r t"),
+                    scalar1=1.0, scalar2=0.0, op0=MULT, op1=ADD,
+                )
+
+        def multiply(i):
+            q0, n = starts[i], CHUNKS[i]
+            codes = mxp.tile([P, 4 * P], U32, name="codes", tag="codes", align_bytes=64)
+            scl = mxp.tile([P, 4 * P], U8, name="scl", tag="scl", align_bytes=64)
+            quantize(state[("grouped", i)], codes, scl, 2 * n)
+            acc = psum_o.tile([P, 4, O], F32, name="acc", tag="acc")
+            for jl in range(2 * n):
                 cols = slice(jl * P, (jl + 1) * P)
                 for w in range(2):
                     nc.tensor.matmul_mx(
@@ -163,104 +169,54 @@ def tile_myinterleavedmodule_t_kernel(tc, x_bytes, x_scale, W_dense, W_sparse, o
                     )
             return acc
 
-        def store(acc, j0, n, on_vector):
-            res = resp.tile([P, MAXT * O], F32, name="res", tag="res")
+        def store(i, acc, on_vector):
+            q0, n = starts[i], CHUNKS[i]
+            res = resp.tile([P, 4 * O], F32, name="res", tag="res")
+            src = acc[:, 0:2 * n].rearrange("p j o -> p (j o)")
             if on_vector:
-                nc.vector.tensor_copy(out=res[:, 0:n * O], in_=acc[:, 0:n, :].rearrange("p j o -> p (j o)"))
+                nc.vector.tensor_copy(out=res[:, 0:2 * n * O], in_=src)
             else:
-                nc.scalar.copy(out=res[:, 0:n * O], in_=acc[:, 0:n, :].rearrange("p j o -> p (j o)"))
-            nc.sync.dma_start(out=out_rows[:, j0 * O:(j0 + n) * O], in_=res[:, 0:n * O])
+                nc.scalar.copy(out=res[:, 0:2 * n * O], in_=src)
+            nc.sync.dma_start(out=out_rows[:, 2 * q0 * O:2 * (q0 + n) * O], in_=res[:, 0:2 * n * O])
 
-        def finish(grouped, j0, n):
-            store(multiply(grouped, n, False), j0, n, False)
+        starts = []
+        q0 = 0
+        for n in CHUNKS:
+            starts.append(q0)
+            q0 += n
+        nchunks = len(CHUNKS)
 
-        def u_cast(q):
-            xc = castp.tile([P, 2 * K], BF16, name="xc", tag="xc")
-            if q < VCAST:
-                nc.vector.tensor_copy(out=xc[:], in_=bytes_of(2 * q, 2).bitcast(FP8))
-            else:
-                nc.scalar.copy(out=xc[:], in_=bytes_of(2 * q, 2).bitcast(FP8))
-            state[("xc", q)] = xc
+        def turn_chunk(i):
+            for q in range(starts[i], starts[i] + CHUNKS[i]):
+                turn(q)
 
-        def u_turn(q):
-            ut = psum_u.tile([P, 2, 2, P], F32, name="ut", tag="ut")
-            turn_bank(ut, state[("xc", q)][:].bitcast(F32), 0, 2)
-            state[("ut", q)] = ut
-
-        def u_tiles(c):
-            return min(MAXT, FIRST - MAXT * c)
-
-        def u_scale(q, t):
-            c = q // 2
-            if q % 2 == 0 and t == 0:
-                pl = planes.tile([P, MAXT * K], BF16, name="pl", tag="pl")
-                state[("pl", c)] = pl
-            nj = u_tiles(c)
-            pl = state[("pl", c)]
-            u, e = divmod(t, 2)
-            j0 = 2 * (q % 2)
-            src = state[("ut", q)][:].rearrange("p j u r -> p (j u r)").bitcast(BF16)
-            src = src.rearrange("p (j u r e) -> p j u r e", j=2, u=2, e=2)
-            dst = pl[:, 0:nj * K].rearrange("p (u j r e) -> p u j r e", u=2, j=nj, e=2)
-            nc.scalar.activation(
-                out=dst[:, u, j0:j0 + 2, :, e], in_=src[:, :, u, :, e], func=COPY, scale=scale_cols[:, t:t + 1]
-            )
-
-        def u_weave(c):
-            nj = u_tiles(c)
-            grouped = grp.tile([P, MAXT * K], BF16, name="grouped", tag="grouped", align_bytes=64)
-            nc.scalar.copy(
-                out=grouped[:, 0:nj * K].bitcast(F32).rearrange("p (j r u) -> p j r u", r=P, u=2),
-                in_=state[("pl", c)][:, 0:nj * K].bitcast(F32).rearrange("p (u j r) -> p j r u", u=2, r=P),
-            )
-            state[("woven", c)] = grouped
-
-        u_cast(0)
-        u_turn(0)
-        u_cast(1)
-        u_turn(1)
-        w_banks = turn(w_sb, 2)
-        for t in range(4):
-            u_scale(0, t)
-        gather(w_banks, w_grouped)
-
-        weave_at = {}
-        for c in range((UNITS + 1) // 2):
-            last_unit = min(2 * c + 1, UNITS - 1)
-            weave_at[2 * last_unit + 3] = c
-
+        for q in range(AHEAD):
+            cast(q)
+        nxt = AHEAD
+        turn_chunk(0)
+        wb = turn_words(w_sb[:])
+        nc.scalar.copy(
+            out=w_grouped[:].bitcast(F32).rearrange("p (m u) -> p m u", u=2),
+            in_=wb[:].rearrange("p u j r -> p (j r) u"),
+        )
         done = 0
         for i in range(nchunks + 1):
             if i < nchunks:
-                stage_a(i)
-                if i == 0:
-                    u_cast(2)
-                stage_b(i)
-                stage_c(i)
-            if i + LAG in weave_at:
-                u_weave(weave_at[i + LAG])
-            q = 1 + i // 2
-            if q < UNITS:
-                u_scale(q, 2 * (i % 2))
-                u_scale(q, 2 * (i % 2) + 1)
-            q = (i + 5) // 2
-            if i % 2 == 1 and 3 <= q < UNITS:
-                u_cast(q)
-            q = (i + 3) // 2
-            if i % 2 == 1 and 2 <= q < UNITS:
-                u_turn(q)
-            if i == LAG:
+                grouped = grp.tile([P, 4 * K], BF16, name="grouped", tag="grouped", align_bytes=64)
+                state[("grouped", i)] = grouped
+                if i + 1 < nchunks:
+                    turn_chunk(i + 1)
+                for g0 in range(CHUNKS[i]):
+                    q = starts[i] + g0
+                    state[("place", q)] = (grouped, g0)
+                    scale(q)
+                    if nxt < PAIRS:
+                        cast(nxt)
+                        nxt += 1
+            if i == 1:
                 quantize(w_grouped, w_codes, w_scl, 2)
-            if i in weave_at:
-                c = weave_at[i]
-                finish(state[("woven", c)], MAXT * c, u_tiles(c))
-            lag = LAG if i < nchunks - TAPER - 1 else LATE_LAGS[i - (nchunks - TAPER - 1)]
-            late = []
+            lag = LAG if i < nchunks else 0
             while done < nchunks and done <= i - lag:
-                if TAILFIX and done >= nchunks - 2:
-                    late.append((multiply(state[("grouped", done)], CHUNKS[done], True), starts[done], CHUNKS[done]))
-                else:
-                    finish(state[("grouped", done)], starts[done], CHUNKS[done])
+                acc = multiply(done)
+                store(done, acc, done == nchunks - 1)
                 done += 1
-            for acc, j0, n in late:
-                store(acc, j0, n, True)

@@ -22,11 +22,16 @@ TILES = ROWS // P
 PAIRS = TILES // 2
 
 CASTS = ["V","S","S","S","S","S","S","S","S","S","S","S","S","S","S","S","S","S","S","S","S","S","S","S","S","S","S","S","S","S","S","S"]
-ROADS = ["p","e","p","e","p","e","p","f","p","e","p","e","p","e","p","f","p","e","p","e","p","e","p","f","p","e","p","e","p","e","p","p"]
-LOADS = [(0, 2), (2, 2), (4, 4), (8, 8), (16, 8), (24, 8), (32, 8), (40, 8), (48, 8), (56, 8)]
-W_AFTER = 2
-LAG = 2
-AHEAD = 4
+ROADS = ["p","e","e","p","p","e","f","p","e","p","p","e","f","p","e","p","p","e","f","p","e","p","p","e","f","p","e","p","p","e","e","p"]
+LOADS = [(0, 1), (1, 1), (2, 2), (4, 4), (8, 8), (16, 8), (24, 8), (32, 8), (40, 8), (48, 8), (56, 8)]
+W_AFTER = 3
+LAG = 3
+WQ = 3
+SPARE = 2
+ORDER = "TSCQ"
+LATE = [1, 1]
+TURN_AHEAD = 2
+AHEAD = 7
 CHUNKS = [2] * 15 + [1, 1]
 
 
@@ -38,13 +43,13 @@ def tile_myinterleavedmodule_t_kernel(tc, x_bytes, x_scale, W_dense, W_sparse, o
     with ExitStack() as ctx:
         const = ctx.enter_context(tc.tile_pool(name="const", bufs=1))
         held = ctx.enter_context(tc.tile_pool(name="held", bufs=1))
-        castp = ctx.enter_context(tc.tile_pool(name="castp", bufs=6))
+        castp = ctx.enter_context(tc.tile_pool(name="castp", bufs=8))
         planep = ctx.enter_context(tc.tile_pool(name="planep", bufs=4))
         grp = ctx.enter_context(tc.tile_pool(name="grp", bufs=5))
         mxp = ctx.enter_context(tc.tile_pool(name="mxp", bufs=3))
         resp = ctx.enter_context(tc.tile_pool(name="resp", bufs=6))
-        psum_t = ctx.enter_context(tc.psum_pool(name="psum_t", bufs=5))
-        psum_o = ctx.enter_context(tc.psum_pool(name="psum_o", bufs=3))
+        psum_t = ctx.enter_context(tc.psum_pool(name="psum_t", bufs=6))
+        psum_o = ctx.enter_context(tc.psum_pool(name="psum_o", bufs=2))
 
         ctx.enter_context(tc.manual_schedule())
 
@@ -103,14 +108,15 @@ def tile_myinterleavedmodule_t_kernel(tc, x_bytes, x_scale, W_dense, W_sparse, o
 
         def cast(q):
             xc = castp.tile([P, 2 * K], BF16, name="xc", tag="xc")
-            src = bytes_of(2 * q, 2).bitcast(FP8)
+            src = bytes_of(2 * q, 2).bitcast(FP8) if CASTS[q] != "V" else None
             if CASTS[q] == "S":
                 nc.scalar.copy(out=xc[:], in_=src)
             elif CASTS[q] == "G":
                 for h in range(2):
                     nc.gpsimd.tensor_copy(out=xc[:, h * K:(h + 1) * K], in_=src[:, h * K:(h + 1) * K])
             else:
-                nc.vector.tensor_copy(out=xc[:], in_=src)
+                for h in range(2):
+                    nc.vector.tensor_copy(out=xc[:, h * K:(h + 1) * K], in_=bytes_of(2 * q + h, 1).bitcast(FP8))
             state[("xc", q)] = xc
 
         def turn(q):
@@ -123,14 +129,31 @@ def tile_myinterleavedmodule_t_kernel(tc, x_bytes, x_scale, W_dense, W_sparse, o
             dst = grouped[:, g0 * 2 * K:(g0 + 1) * 2 * K]
             if ROADS[q] == "p":
                 src = bank[:].rearrange("p u j r -> p (u j r)").bitcast(BF16)
-                nc.vector.tensor_tensor(
-                    out=dst.rearrange("p (m u e) -> p m u e", u=2, e=2),
-                    in0=src.rearrange("p (u m e) -> p m u e", u=2, e=2),
-                    in1=scale_cols[:].to_broadcast([P, 2 * P, 2, 2]),
-                    op=MULT,
-                )
+                parts = 2 if q == 0 else 1
+                m = 2 * P // parts
+                for h in range(parts):
+                    nc.vector.tensor_tensor(
+                        out=dst[:, h * 4 * m:(h + 1) * 4 * m].rearrange("p (m u e) -> p m u e", u=2, e=2),
+                        in0=src.rearrange("p (u m e) -> p m u e", u=2, e=2)[:, h * m:(h + 1) * m],
+                        in1=scale_cols[:].to_broadcast([P, m, 2, 2]),
+                        op=MULT,
+                    )
                 return
             pl = planep.tile([P, 4, 2 * P], BF16, name="pl", tag="pl")
+            if ROADS[q] == "u":
+                flat = pl[:].rearrange("p t m -> p (t m)")
+                pairs = flat.rearrange("p (u m e) -> p u e m", u=2, e=2)
+                src = bank[:].rearrange("p u j r -> p (u j r)").bitcast(BF16)
+                src = src.rearrange("p (u m e) -> p u e m", u=2, e=2)
+                for t in range(4):
+                    nc.scalar.activation(
+                        out=pairs[:, t // 2, t % 2, :], in_=src[:, t // 2, t % 2, :], func=COPY, scale=flat_cols[:, t:t + 1]
+                    )
+                nc.scalar.copy(
+                    out=dst.bitcast(F32).rearrange("p (m u) -> p m u", u=2),
+                    in_=flat.bitcast(F32).rearrange("p (u m) -> p m u", u=2),
+                )
+                return
             if ROADS[q] == "e":
                 for t in range(4):
                     nc.vector.tensor_scalar(
@@ -142,19 +165,21 @@ def tile_myinterleavedmodule_t_kernel(tc, x_bytes, x_scale, W_dense, W_sparse, o
                 src = src.rearrange("p (u m e) -> p u e m", u=2, e=2)
                 for t in range(4):
                     nc.scalar.activation(out=pl[:, t, :], in_=src[:, t // 2, t % 2, :], func=COPY, scale=flat_cols[:, t:t + 1])
-            for h in range(2):
-                nc.gpsimd.tensor_scalar(
-                    out=dst[:, h * K:(h + 1) * K].rearrange("p (r t) -> p r t", t=4),
-                    in0=pl[:, :, h * P:(h + 1) * P].rearrange("p t r -> p r t"),
-                    scalar1=1.0, scalar2=0.0, op0=MULT, op1=ADD,
-                )
+            nc.gpsimd.tensor_scalar(
+                out=dst.rearrange("p (m t) -> p m t", t=4),
+                in0=pl[:].rearrange("p t m -> p m t"),
+                scalar1=1.0, scalar2=0.0, op0=MULT, op1=ADD,
+            )
 
         def multiply(i):
             q0, n = starts[i], CHUNKS[i]
             codes = mxp.tile([P, 4 * P], U32, name="codes", tag="codes", align_bytes=64)
             scl = mxp.tile([P, 4 * P], U8, name="scl", tag="scl", align_bytes=64)
             quantize(state[("grouped", i)], codes, scl, 2 * n)
-            acc = psum_o.tile([P, 4, O], F32, name="acc", tag="acc")
+            if i >= nchunks - SPARE:
+                acc = psum_t.tile([P, 4, O], F32, name="last", tag="bank")
+            else:
+                acc = psum_o.tile([P, 4, O], F32, name="acc", tag="acc")
             for jl in range(2 * n):
                 cols = slice(jl * P, (jl + 1) * P)
                 for w in range(2):
@@ -193,30 +218,39 @@ def tile_myinterleavedmodule_t_kernel(tc, x_bytes, x_scale, W_dense, W_sparse, o
         for q in range(AHEAD):
             cast(q)
         nxt = AHEAD
-        turn_chunk(0)
+        for i in range(TURN_AHEAD):
+            turn_chunk(i)
         wb = turn_words(w_sb[:])
         nc.scalar.copy(
             out=w_grouped[:].bitcast(F32).rearrange("p (m u) -> p m u", u=2),
             in_=wb[:].rearrange("p u j r -> p (j r) u"),
         )
+        VSTORE = (nchunks - 1,)
         done = 0
         for i in range(nchunks + 1):
             if i < nchunks:
                 grouped = grp.tile([P, 4 * K], BF16, name="grouped", tag="grouped", align_bytes=64)
                 state[("grouped", i)] = grouped
-                if i + 1 < nchunks:
-                    turn_chunk(i + 1)
-                for g0 in range(CHUNKS[i]):
-                    q = starts[i] + g0
-                    state[("place", q)] = (grouped, g0)
-                    scale(q)
-                    if nxt < PAIRS:
-                        cast(nxt)
-                        nxt += 1
-            if i == 1:
+            if i == WQ:
                 quantize(w_grouped, w_codes, w_scl, 2)
-            lag = LAG if i < nchunks else 0
-            while done < nchunks and done <= i - lag:
-                acc = multiply(done)
-                store(done, acc, done == nchunks - 1)
-                done += 1
+            for act in ORDER:
+                if act == "T" and i + TURN_AHEAD < nchunks:
+                    turn_chunk(i + TURN_AHEAD)
+                if act == "S" and i < nchunks:
+                    for g0 in range(CHUNKS[i]):
+                        q = starts[i] + g0
+                        state[("place", q)] = (grouped, g0)
+                        scale(q)
+                if act == "C":
+                    for k in range(CHUNKS[min(i, nchunks - 1)]):
+                        if nxt < PAIRS:
+                            cast(nxt)
+                            nxt += 1
+                if act == "Q":
+                    lag = LAG if i < nchunks - len(LATE) else LATE[min(i - nchunks + len(LATE), len(LATE) - 1)]
+                    if i == nchunks:
+                        lag = 0
+                    while done < nchunks and done <= i - lag:
+                        acc = multiply(done)
+                        store(done, acc, done in VSTORE)
+                        done += 1

@@ -22,17 +22,17 @@ TILES = ROWS // P
 PAIRS = TILES // 2
 
 CASTS = ["V","S","S","S","S","S","S","S","S","S","S","S","S","S","S","S","S","S","S","S","S","S","S","S","S","S","S","S","S","S","S","S"]
-ROADS = ["p","e","e","p","p","e","f","p","e","p","p","e","f","p","e","p","p","e","f","p","e","p","p","e","f","p","e","p","p","e","e","p"]
+ROADS = ["p","e","p","p","e","f","p","p","e","f","p","p","e","f","p","p","e","f","p","p","e","f","p","p","e","f","p","p","p","p","p","p"]
 LOADS = [(0, 1), (1, 1), (2, 2), (4, 4), (8, 8), (16, 8), (24, 8), (32, 8), (40, 8), (48, 8), (56, 8)]
 W_AFTER = 3
 LAG = 3
 WQ = 3
-SPARE = 2
+SPARE = 3
 ORDER = "TSCQ"
 LATE = [1, 1]
 TURN_AHEAD = 2
 AHEAD = 7
-CHUNKS = [2] * 15 + [1, 1]
+CHUNKS = [1, 1] + [2] * 13 + [1] * 4
 
 
 def tile_myinterleavedmodule_t_kernel(tc, x_bytes, x_scale, W_dense, W_sparse, out):

@@ -22,17 +22,17 @@ TILES = ROWS // P
 PAIRS = TILES // 2
 
 CASTS = ["V","S","S","S","S","S","S","S","S","S","S","S","S","S","S","S","S","S","S","S","S","S","S","S","S","S","S","S","S","S","S","S"]
-ROADS = ["p","e","p","p","e","f","p","p","e","f","p","p","e","f","p","p","e","f","p","p","e","f","p","p","e","f","p","p","p","p","p","p"]
+ROADS = ["p","e","p","f","p","e","p","f","p","e","p","f","p","e","p","f","p","e","p","f","p","e","p","f","p","e","p","f","p","e","p","p"]
 LOADS = [(0, 1), (1, 1), (2, 2), (4, 4), (8, 8), (16, 8), (24, 8), (32, 8), (40, 8), (48, 8), (56, 8)]
 W_AFTER = 3
 LAG = 3
 WQ = 3
 SPARE = 3
 ORDER = "TSCQ"
-LATE = [1, 1]
+LATE = [2, 1]
 TURN_AHEAD = 2
 AHEAD = 7
-CHUNKS = [1, 1] + [2] * 13 + [1] * 4
+CHUNKS = [2] * 14 + [1] * 4
 
 
 def tile_myinterleavedmodule_t_kernel(tc, x_bytes, x_scale, W_dense, W_sparse, out):

from contextlib import ExitStack

import concourse.mybir as mybir
from concourse.masks import make_identity

ROWS, K, O = 8192, 512, 128
FLOPS = 2 * 2 * ROWS * K * O

F32 = mybir.dt.float32
BF16 = mybir.dt.bfloat16
U32 = mybir.dt.uint32
U8 = mybir.dt.uint8
FP8 = mybir.dt.float8_e4m3fn
FP8X4 = mybir.dt.float8_e4m3fn_x4

COPY = mybir.ActivationFunctionType.Copy
MULT = mybir.AluOpType.mult
ADD = mybir.AluOpType.add

P = 128
TILES = ROWS // P
PAIRS = TILES // 2

CASTS = ["V","S","S","S","S","S","S","S","S","S","S","S","S","S","S","S","S","S","S","S","S","S","S","S","S","S","S","S","S","S","S","S"]
ROADS = ["p","e","p","f","p","e","p","f","p","e","p","f","p","e","p","f","p","e","p","f","p","e","p","f","p","e","p","f","p","e","p","p"]
LOADS = [(0, 1), (1, 1), (2, 2), (4, 4), (8, 8), (16, 8), (24, 8), (32, 8), (40, 8), (48, 8), (56, 8)]
W_AFTER = 3
LAG = 3
WQ = 3
SPARE = 3
ORDER = "TSCQ"
LATE = [2, 1]
TURN_AHEAD = 2
AHEAD = 7
CHUNKS = [2] * 14 + [1] * 4


def tile_myinterleavedmodule_t_kernel(tc, x_bytes, x_scale, W_dense, W_sparse, out):
    nc = tc.nc
    x_rows = x_bytes.rearrange("(p j) k -> p (j k)", j=TILES)
    out_rows = out.rearrange("(p j) o -> p (j o)", j=TILES)

    with ExitStack() as ctx:
        const = ctx.enter_context(tc.tile_pool(name="const", bufs=1))
        held = ctx.enter_context(tc.tile_pool(name="held", bufs=1))
        castp = ctx.enter_context(tc.tile_pool(name="castp", bufs=8))
        planep = ctx.enter_context(tc.tile_pool(name="planep", bufs=4))
        grp = ctx.enter_context(tc.tile_pool(name="grp", bufs=5))
        mxp = ctx.enter_context(tc.tile_pool(name="mxp", bufs=3))
        resp = ctx.enter_context(tc.tile_pool(name="resp", bufs=6))
        psum_t = ctx.enter_context(tc.psum_pool(name="psum_t", bufs=6))
        psum_o = ctx.enter_context(tc.psum_pool(name="psum_o", bufs=2))

        ctx.enter_context(tc.manual_schedule())

        ident = const.tile([P, P], F32, name="ident")
        make_identity(nc, ident[:])
        ident_b = const.tile([P, P], BF16, name="ident_b")
        nc.vector.tensor_copy(out=ident_b[:], in_=ident[:])

        scale_cols = const.tile([P, 1, 2, 2], F32, name="scale_cols")
        nc.scalar.dma_start(out=scale_cols[:].rearrange("p o u e -> p (o u e)"), in_=x_scale.rearrange("o (p t) -> p (o t)", t=4))
        flat_cols = scale_cols[:].rearrange("p o u e -> p (o u e)")
        warm = const.tile([P, 1], F32, name="warm")
        nc.scalar.activation(out=warm[:], in_=ident[:, 0:1], func=COPY)

        w_sb = const.tile([P, 2 * K], BF16, name="w_sb")
        byte_tiles = []
        for g, (start, n) in enumerate(LOADS):
            xb = held.tile([P, n * K], U8, name="xbytes%d" % g)
            nc.sync.dma_start(out=xb[:], in_=x_rows[:, start * K:(start + n) * K])
            byte_tiles.append((start, n, xb))
            if g == W_AFTER:
                nc.sync.dma_start(out=w_sb[:, 0:K], in_=W_dense)
                nc.sync.dma_start(out=w_sb[:, K:2 * K], in_=W_sparse)

        def bytes_of(j0, n):
            for s, m, xb in byte_tiles:
                if s <= j0 and j0 + n <= s + m:
                    return xb[:, (j0 - s) * K:(j0 - s + n) * K]
            raise ValueError("pair crosses a load")

        def turn_words(src):
            words = src.bitcast(F32)
            bank = psum_t.tile([P, 2, 2, P], F32, name="bank", tag="bank")
            for j in range(2):
                for u in range(2):
                    nc.tensor.transpose(bank[:, u, j, :], words[:, j * 256 + u:(j + 1) * 256:2], ident[:])
            return bank

        def turn_values(src):
            bank = psum_t.tile([P, 4, 2, P], BF16, name="bankb", tag="bank")
            for j in range(2):
                for t in range(4):
                    nc.tensor.transpose(bank[:, t, j, :], src[:, j * K + t:(j + 1) * K:4], ident_b[:])
            return bank

        def quantize(grouped, codes, scl, n):
            nc.vector.quantize_mx(
                out=codes[:, 0:n * P].bitcast(FP8X4), scales=scl[:, 0:n * P], in_=grouped[:, 0:n * K]
            )

        w_grouped = const.tile([P, 2 * K], BF16, name="w_grouped", align_bytes=64)
        w_codes = const.tile([P, 2 * P], U32, name="w_codes", align_bytes=64)
        w_scl = const.tile([P, 2 * P], U8, name="w_scl", align_bytes=64)

        state = {}

        def cast(q):
            xc = castp.tile([P, 2 * K], BF16, name="xc", tag="xc")
            src = bytes_of(2 * q, 2).bitcast(FP8) if CASTS[q] != "V" else None
            if CASTS[q] == "S":
                nc.scalar.copy(out=xc[:], in_=src)
            elif CASTS[q] == "G":
                for h in range(2):
                    nc.gpsimd.tensor_copy(out=xc[:, h * K:(h + 1) * K], in_=src[:, h * K:(h + 1) * K])
            else:
                for h in range(2):
                    nc.vector.tensor_copy(out=xc[:, h * K:(h + 1) * K], in_=bytes_of(2 * q + h, 1).bitcast(FP8))
            state[("xc", q)] = xc

        def turn(q):
            xc = state[("xc", q)]
            state[("bank", q)] = turn_values(xc[:]) if ROADS[q] == "e" else turn_words(xc[:])

        def scale(q):
            bank = state[("bank", q)]
            grouped, g0 = state[("place", q)]
            dst = grouped[:, g0 * 2 * K:(g0 + 1) * 2 * K]
            if ROADS[q] == "p":
                src = bank[:].rearrange("p u j r -> p (u j r)").bitcast(BF16)
                parts = 2 if q == 0 else 1
                m = 2 * P // parts
                for h in range(parts):
                    nc.vector.tensor_tensor(
                        out=dst[:, h * 4 * m:(h + 1) * 4 * m].rearrange("p (m u e) -> p m u e", u=2, e=2),
                        in0=src.rearrange("p (u m e) -> p m u e", u=2, e=2)[:, h * m:(h + 1) * m],
                        in1=scale_cols[:].to_broadcast([P, m, 2, 2]),
                        op=MULT,
                    )
                return
            pl = planep.tile([P, 4, 2 * P], BF16, name="pl", tag="pl")
            if ROADS[q] == "u":
                flat = pl[:].rearrange("p t m -> p (t m)")
                pairs = flat.rearrange("p (u m e) -> p u e m", u=2, e=2)
                src = bank[:].rearrange("p u j r -> p (u j r)").bitcast(BF16)
                src = src.rearrange("p (u m e) -> p u e m", u=2, e=2)
                for t in range(4):
                    nc.scalar.activation(
                        out=pairs[:, t // 2, t % 2, :], in_=src[:, t // 2, t % 2, :], func=COPY, scale=flat_cols[:, t:t + 1]
                    )
                nc.scalar.copy(
                    out=dst.bitcast(F32).rearrange("p (m u) -> p m u", u=2),
                    in_=flat.bitcast(F32).rearrange("p (u m) -> p m u", u=2),
                )
                return
            if ROADS[q] == "e":
                for t in range(4):
                    nc.vector.tensor_scalar(
                        out=pl[:, t, :], in0=bank[:, t].rearrange("p j r -> p (j r)"),
                        scalar1=flat_cols[:, t:t + 1], scalar2=None, op0=MULT,
                    )
            else:
                src = bank[:].rearrange("p u j r -> p (u j r)").bitcast(BF16)
                src = src.rearrange("p (u m e) -> p u e m", u=2, e=2)
                for t in range(4):
                    nc.scalar.activation(out=pl[:, t, :], in_=src[:, t // 2, t % 2, :], func=COPY, scale=flat_cols[:, t:t + 1])
            nc.gpsimd.tensor_scalar(
                out=dst.rearrange("p (m t) -> p m t", t=4),
                in0=pl[:].rearrange("p t m -> p m t"),
                scalar1=1.0, scalar2=0.0, op0=MULT, op1=ADD,
            )

        def multiply(i):
            q0, n = starts[i], CHUNKS[i]
            codes = mxp.tile([P, 4 * P], U32, name="codes", tag="codes", align_bytes=64)
            scl = mxp.tile([P, 4 * P], U8, name="scl", tag="scl", align_bytes=64)
            quantize(state[("grouped", i)], codes, scl, 2 * n)
            if i >= nchunks - SPARE:
                acc = psum_t.tile([P, 4, O], F32, name="last", tag="bank")
            else:
                acc = psum_o.tile([P, 4, O], F32, name="acc", tag="acc")
            for jl in range(2 * n):
                cols = slice(jl * P, (jl + 1) * P)
                for w in range(2):
                    nc.tensor.matmul_mx(
                        out=acc[:, jl, :],
                        lhsT=codes[:, cols].bitcast(FP8X4),
                        lhsT_scale=scl[:, cols],
                        rhs=w_codes[:, w * O:(w + 1) * O].bitcast(FP8X4),
                        rhs_scale=w_scl[:, w * O:(w + 1) * O],
                        start=(w == 0),
                        stop=(w == 1),
                    )
            return acc

        def store(i, acc, on_vector):
            q0, n = starts[i], CHUNKS[i]
            res = resp.tile([P, 4 * O], F32, name="res", tag="res")
            src = acc[:, 0:2 * n].rearrange("p j o -> p (j o)")
            if on_vector:
                nc.vector.tensor_copy(out=res[:, 0:2 * n * O], in_=src)
            else:
                nc.scalar.copy(out=res[:, 0:2 * n * O], in_=src)
            nc.sync.dma_start(out=out_rows[:, 2 * q0 * O:2 * (q0 + n) * O], in_=res[:, 0:2 * n * O])

        starts = []
        q0 = 0
        for n in CHUNKS:
            starts.append(q0)
            q0 += n
        nchunks = len(CHUNKS)

        def turn_chunk(i):
            for q in range(starts[i], starts[i] + CHUNKS[i]):
                turn(q)

        for q in range(AHEAD):
            cast(q)
        nxt = AHEAD
        for i in range(TURN_AHEAD):
            turn_chunk(i)
        wb = turn_words(w_sb[:])
        nc.scalar.copy(
            out=w_grouped[:].bitcast(F32).rearrange("p (m u) -> p m u", u=2),
            in_=wb[:].rearrange("p u j r -> p (j r) u"),
        )
        VSTORE = (nchunks - 1,)
        done = 0
        for i in range(nchunks + 1):
            if i < nchunks:
                grouped = grp.tile([P, 4 * K], BF16, name="grouped", tag="grouped", align_bytes=64)
                state[("grouped", i)] = grouped
            if i == WQ:
                quantize(w_grouped, w_codes, w_scl, 2)
            for act in ORDER:
                if act == "T" and i + TURN_AHEAD < nchunks:
                    turn_chunk(i + TURN_AHEAD)
                if act == "S" and i < nchunks:
                    for g0 in range(CHUNKS[i]):
                        q = starts[i] + g0
                        state[("place", q)] = (grouped, g0)
                        scale(q)
                if act == "C":
                    for k in range(CHUNKS[min(i, nchunks - 1)]):
                        if nxt < PAIRS:
                            cast(nxt)
                            nxt += 1
                if act == "Q":
                    lag = LAG if i < nchunks - len(LATE) else LATE[min(i - nchunks + len(LATE), len(LATE) - 1)]
                    if i == nchunks:
                        lag = 0
                    while done < nchunks and done <= i - lag:
                        acc = multiply(done)
                        store(done, acc, done in VSTORE)
                        done += 1
